import numpy as np
import ml_dtypes


def mxq(x, axis, fmt="e4m3"):
    dtype, down = {"e4m3": (ml_dtypes.float8_e4m3fn, 7), "e5m2": (ml_dtypes.float8_e5m2, 14)}[fmt]
    v = np.moveaxis(np.asarray(x, np.float32).astype(ml_dtypes.bfloat16).astype(np.float64), axis, -1)
    blocks = v.reshape(v.shape[:-1] + (-1, 32))
    amax = np.abs(blocks).max(-1, keepdims=True)
    byte = np.maximum(np.where(amax > 0, np.frexp(amax)[1] - 1 + 127, 0) - down, 1)
    scale = np.exp2(byte - 127.0)
    codes = (blocks / scale).astype(np.float32).astype(dtype).astype(np.float64)
    return np.moveaxis((codes * scale).reshape(v.shape), -1, axis)


WIDE = False


def mx_kscale(k):
    if not WIDE:
        return np.ones(k)
    levels = np.array([10, -10, 5, -5, 0])
    if k % 512:
        return np.exp2(np.random.permutation(np.resize(levels, k // 32))).repeat(32)
    a = np.empty((k // 512, 16))
    for p in range(k // 512):
        a[p, :8] = np.random.permutation(np.resize(levels, 8))
        for g in range(8):
            far = levels[np.abs(levels - a[p, g]) >= 10]
            a[p, g + 8] = far[np.random.randint(len(far))]
    return np.exp2(a.ravel()).repeat(32)


BF16 = ml_dtypes.bfloat16


def bf(x):
    return np.asarray(x, np.float32).astype(BF16)


def f64(x):
    return np.asarray(x).astype(np.float64)


B, D_IN, D_H = 4096, 512, 512


def sigmoid(v):
    return 1.0 / (1.0 + np.exp(-v))


def setup_inputs():
    s, t = mx_kscale(D_IN), mx_kscale(D_H)

    def w_in():
        return bf(np.random.standard_normal((D_H, D_IN)) * 0.6 / np.sqrt(D_IN) / s[None, :])

    def w_rec():
        return bf(np.random.standard_normal((D_H, D_H)) * 0.6 / np.sqrt(D_H) / t[None, :])

    def bias():
        return bf(np.random.standard_normal(D_H) * 0.3)

    return {"incoming": bf(np.random.standard_normal((B, D_IN)) * s), "h": bf(np.random.standard_normal((B, D_H)) * t),
            "W_i": w_in(), "b_W_i": bias(), "W_c": w_in(), "b_W_c": bias(),
            "U_i": w_rec(), "b_U_i": bias(), "U_c": w_rec(), "b_U_c": bias()}


def reference(incoming, h, W_i, b_W_i, W_c, b_W_c, U_i, b_U_i, U_c, b_U_c):
    xq = mxq(f64(incoming), 1, "e4m3")
    hq = mxq(f64(h), 1, "e4m3")
    I = sigmoid((xq @ mxq(f64(W_i), 1, "e4m3").T) + f64(b_W_i) + (hq @ mxq(f64(U_i), 1, "e4m3").T) + f64(b_U_i))
    C_head = (xq @ mxq(f64(W_c), 1, "e4m3").T) + f64(b_W_c) + (hq @ mxq(f64(U_c), 1, "e4m3").T) + f64(b_U_c)
    return I * C_head

@@ -1,0 +1,182 @@
+from contextlib import ExitStack
+
+import concourse.masks as masks
+import concourse.mybir as mybir
+
+F32 = mybir.dt.float32
+BF16 = mybir.dt.bfloat16
+U32 = mybir.dt.uint32
+U8 = mybir.dt.uint8
+FP8X4 = mybir.dt.float8_e4m3fn_x4
+ADD = mybir.AluOpType.add
+MULT = mybir.AluOpType.mult
+SIGMOID = mybir.ActivationFunctionType.Sigmoid
+
+P = 128
+BATCH = 4096
+K = 512
+D_H = 512
+PAIR = 2
+PAIR_ROWS = PAIR * P
+PAIR_WORDS = PAIR * K // 2
+N_ROUNDS = BATCH // PAIR_ROWS
+
+FLOPS = 2 * BATCH * K * D_H * 4
+
+
+def tile_lstmcell_pa_t_kernel(
+    tc, incoming, h, W_i, b_W_i, W_c, b_W_c, U_i, b_U_i, U_c, b_U_c, out
+):
+    nc = tc.nc
+    with ExitStack() as ctx:
+        consts = ctx.enter_context(tc.tile_pool(name="consts", bufs=1))
+        acts = ctx.enter_context(tc.tile_pool(name="acts", bufs=N_ROUNDS))
+        w_stage = ctx.enter_context(tc.tile_pool(name="w_stage", bufs=4))
+        quant = ctx.enter_context(tc.tile_pool(name="quant", bufs=3))
+        gates = ctx.enter_context(tc.tile_pool(name="gates", bufs=4))
+        results = ctx.enter_context(tc.tile_pool(name="results", bufs=10))
+        words_psum = ctx.enter_context(tc.psum_pool(name="words_psum", bufs=4))
+        sums_psum = ctx.enter_context(tc.psum_pool(name="sums_psum", bufs=2))
+        ctx.enter_context(tc.manual_schedule())
+
+        ident = consts.tile([P, P], F32)
+        masks.make_identity(nc, ident[:])
+        ones = consts.tile([P, P], BF16)
+        nc.vector.memset(ones[:], 1.0)
+        bias_rows = consts.tile([P, 2 * D_H], BF16)
+        nc.vector.memset(bias_rows[:], 0.0)
+        for row, (b_i, b_c) in enumerate(((b_W_i, b_W_c), (b_U_i, b_U_c))):
+            nc.scalar.dma_start(out=bias_rows[row : row + 1, 0:D_H], in_=b_i.unsqueeze(0))
+            nc.scalar.dma_start(out=bias_rows[row : row + 1, D_H : 2 * D_H], in_=b_c.unsqueeze(0))
+        table_warmer = consts.tile([P, 1], F32)
+        nc.vector.memset(table_warmer[:], 0.0)
+        nc.scalar.activation(out=table_warmer[:], in_=table_warmer[:], func=SIGMOID)
+
+        x_view = incoming.rearrange("(n p i) k -> n p (i k)", p=P, i=PAIR)
+        h_view = h.rearrange("(n p i) k -> n p (i k)", p=P, i=PAIR)
+        out_view = out.rearrange("(n p i) f -> n p i f", p=P, i=PAIR)
+        act_words = []
+
+        def load_round(n):
+            x_rows = acts.tile([P, PAIR * K], BF16)
+            nc.sync.dma_start(out=x_rows[:], in_=x_view[n])
+            h_rows = acts.tile([P, PAIR * K], BF16)
+            nc.sync.dma_start(out=h_rows[:], in_=h_view[n])
+            act_words.append((x_rows[:].bitcast(F32), h_rows[:].bitcast(F32)))
+
+        load_round(0)
+        weight_words = []
+        for w in (W_i, U_i, W_c, U_c):
+            w_rows = w_stage.tile([P, (D_H // P) * K], BF16)
+            nc.sync.dma_start(
+                out=w_rows[:].rearrange("p (r k) -> p r k", k=K),
+                in_=w.rearrange("(r p) k -> p r k", p=P),
+            )
+            weight_words.append(w_rows[:].bitcast(F32))
+        for n in range(1, N_ROUNDS):
+            load_round(n)
+
+        def transpose_pair(words):
+            bank = words_psum.tile([P, 2, PAIR_ROWS], F32)
+            for s in range(PAIR):
+                for u in range(2):
+                    nc.tensor.transpose(
+                        out=bank[:, u, s * P : (s + 1) * P],
+                        in_=words[:, 2 * s * P + u : 2 * (s + 1) * P : 2],
+                        identity=ident[:],
+                    )
+            return bank
+
+        def regroup(copy, bank, grouped, b):
+            copy(
+                out=grouped[:]
+                .bitcast(F32)[:, b * PAIR_WORDS : (b + 1) * PAIR_WORDS]
+                .rearrange("p (r u) -> p r u", u=2),
+                in_=bank[:].rearrange("p u r -> p r u"),
+            )
+
+        word_banks = {}
+        grouped_tiles = {}
+        packed = {}
+
+        def transpose_round(n):
+            word_banks[n] = [transpose_pair(words) for words in act_words[n]]
+            grouped = quant.tile([P, 2 * PAIR_ROWS * 4], BF16, align_bytes=64)
+            grouped_tiles[n] = grouped
+
+        def regroup_operand(n, operand):
+            regroup(nc.scalar.copy, word_banks[n][operand], grouped_tiles[n], operand)
+
+        def quantise_round(n):
+            codes = quant.tile([P, 2 * PAIR_ROWS], U32, align_bytes=64)
+            scales = quant.tile([P, 2 * PAIR_ROWS], U8, align_bytes=64)
+            nc.vector.quantize_mx(
+                out=codes[:].bitcast(FP8X4), scales=scales[:], in_=grouped_tiles[n][:]
+            )
+            packed[n] = (codes, scales)
+
+        def gate_sums(n, i, gate):
+            codes, scales = packed[n]
+            sums = sums_psum.tile([P, D_H], F32, tag="sums_%d" % gate)
+            for operand in range(2):
+                rows = slice((operand * PAIR + i) * P, (operand * PAIR + i + 1) * P)
+                nc.tensor.matmul_mx(
+                    out=sums[:],
+                    lhsT=codes[:, rows].bitcast(FP8X4),
+                    lhsT_scale=scales[:, rows],
+                    rhs=w_codes[:, 2 * gate + operand, :].bitcast(FP8X4),
+                    rhs_scale=w_scales[:, 2 * gate + operand, :],
+                    start=(operand == 0),
+                    stop=(operand == 1),
+                )
+            return sums
+
+        transpose_round(0)
+        for operand in range(2):
+            regroup_operand(0, operand)
+
+        bias = consts.tile([P, 2, D_H], F32)
+        for gate in range(2):
+            spread = sums_psum.tile([P, D_H], F32, tag="sums_%d" % gate)
+            nc.tensor.matmul(
+                out=spread[:],
+                lhsT=ones[:],
+                rhs=bias_rows[:, gate * D_H : (gate + 1) * D_H],
+                start=True,
+                stop=True,
+            )
+            nc.vector.tensor_copy(out=bias[:, gate, :], in_=spread[:])
+        quantise_round(0)
+
+        w_codes = consts.tile([P, 4, D_H], U32, align_bytes=64)
+        w_scales = consts.tile([P, 4, D_H], U8, align_bytes=64)
+        for m in range(4):
+            w_grouped = w_stage.tile([P, D_H * 4], BF16, align_bytes=64)
+            for b, copy in enumerate((nc.scalar.copy, nc.vector.tensor_copy)):
+                bank = transpose_pair(weight_words[m][:, b * PAIR_WORDS : (b + 1) * PAIR_WORDS])
+                regroup(copy, bank, w_grouped, b)
+            nc.vector.quantize_mx(
+                out=w_codes[:, m, :].bitcast(FP8X4), scales=w_scales[:, m, :], in_=w_grouped[:]
+            )
+
+        transpose_round(1)
+        for operand in range(2):
+            regroup_operand(1, operand)
+
+        for n in range(N_ROUNDS):
+            if n + 1 < N_ROUNDS:
+                quantise_round(n + 1)
+            sums = [(gate_sums(n, 0, 0), gate_sums(n, 0, 1))]
+            if n + 2 < N_ROUNDS:
+                transpose_round(n + 2)
+            sums.append((gate_sums(n, 1, 0), gate_sums(n, 1, 1)))
+            for i, (sums_i, sums_c) in enumerate(sums):
+                gate_i = gates.tile([P, D_H], F32)
+                nc.vector.tensor_tensor(out=gate_i[:], in0=sums_i[:], in1=bias[:, 0, :], op=ADD)
+                if n + 2 < N_ROUNDS:
+                    regroup_operand(n + 2, i)
+                nc.scalar.activation(out=gate_i[:], in_=gate_i[:], func=SIGMOID)
+                result = results.tile([P, D_H], F32)
+                nc.vector.tensor_tensor(out=result[:], in0=sums_c[:], in1=bias[:, 1, :], op=ADD)
+                nc.gpsimd.tensor_tensor(out=result[:], in0=result[:], in1=gate_i[:], op=MULT)
+                nc.sync.dma_start(out=out_view[n, :, i, :], in_=result[:])

@@ -55,26 +55,31 @@ def tile_lstmcell_pa_t_kernel(
         x_view = incoming.rearrange("(n p i) k -> n p (i k)", p=P, i=PAIR)
         h_view = h.rearrange("(n p i) k -> n p (i k)", p=P, i=PAIR)
         out_view = out.rearrange("(n p i) f -> n p i f", p=P, i=PAIR)
-        act_words = []
+        act_words = {}
 
-        def load_round(n):
-            x_rows = acts.tile([P, PAIR * K], BF16)
-            nc.sync.dma_start(out=x_rows[:], in_=x_view[n])
-            h_rows = acts.tile([P, PAIR * K], BF16)
-            nc.sync.dma_start(out=h_rows[:], in_=h_view[n])
-            act_words.append((x_rows[:].bitcast(F32), h_rows[:].bitcast(F32)))
+        def load_operand(n, operand):
+            rows = acts.tile([P, PAIR * K], BF16, name="rows_%d" % operand)
+            nc.sync.dma_start(out=rows[:], in_=(x_view, h_view)[operand][n])
+            act_words.setdefault(n, []).append(rows[:].bitcast(F32))
 
-        load_round(0)
         weight_words = []
-        for w in (W_i, U_i, W_c, U_c):
+
+        def load_weight(w):
             w_rows = w_stage.tile([P, (D_H // P) * K], BF16)
             nc.sync.dma_start(
                 out=w_rows[:].rearrange("p (r k) -> p r k", k=K),
                 in_=w.rearrange("(r p) k -> p r k", p=P),
             )
             weight_words.append(w_rows[:].bitcast(F32))
-        for n in range(1, N_ROUNDS):
-            load_round(n)
+
+        for n in range(N_ROUNDS):
+            load_operand(n, 0)
+            if n == 0:
+                load_weight(W_i)
+            load_operand(n, 1)
+            if n == 0:
+                for w in (U_i, W_c, U_c):
+                    load_weight(w)
 
         def transpose_pair(words):
             bank = words_psum.tile([P, 2, PAIR_ROWS], F32)
@@ -99,71 +104,159 @@ def tile_lstmcell_pa_t_kernel(
         grouped_tiles = {}
         packed = {}
 
+        def new_round(n):
+            word_banks[n] = {}
+            grouped_tiles[n] = quant.tile(
+                [P, 2 * PAIR_ROWS * 4], BF16, align_bytes=64, name="grouped"
+            )
+            codes = quant.tile([P, 2 * PAIR_ROWS], U32, align_bytes=64)
+            scales = quant.tile([P, 2 * PAIR_ROWS], U8, align_bytes=64)
+            packed[n] = (codes, scales)
+
+        def transpose_operand(n, operand):
+            word_banks[n][operand] = transpose_pair(act_words[n][operand])
+
         def transpose_round(n):
-            word_banks[n] = [transpose_pair(words) for words in act_words[n]]
-            grouped = quant.tile([P, 2 * PAIR_ROWS * 4], BF16, align_bytes=64)
-            grouped_tiles[n] = grouped
+            new_round(n)
+            for operand in range(2):
+                transpose_operand(n, operand)
 
         def regroup_operand(n, operand):
             regroup(nc.scalar.copy, word_banks[n][operand], grouped_tiles[n], operand)
 
-        def quantise_round(n):
-            codes = quant.tile([P, 2 * PAIR_ROWS], U32, align_bytes=64)
-            scales = quant.tile([P, 2 * PAIR_ROWS], U8, align_bytes=64)
-            nc.vector.quantize_mx(
-                out=codes[:].bitcast(FP8X4), scales=scales[:], in_=grouped_tiles[n][:]
-            )
-            packed[n] = (codes, scales)
-
-        def gate_sums(n, i, gate):
+        def quantise(n, first, last):
             codes, scales = packed[n]
+            cols = slice(first * PAIR_ROWS, (last + 1) * PAIR_ROWS)
+            nc.vector.quantize_mx(
+                out=codes[:, cols].bitcast(FP8X4),
+                scales=scales[:, cols],
+                in_=grouped_tiles[n][:, cols.start * 4 : cols.stop * 4],
+            )
+
+        def quantise_round(n):
+            quantise(n, 0, 1)
+
+        def multiply(sums, n, i, gate, operand):
+            codes, scales = packed[n]
+            rows = slice((operand * PAIR + i) * P, (operand * PAIR + i + 1) * P)
+            nc.tensor.matmul_mx(
+                out=sums[:],
+                lhsT=codes[:, rows].bitcast(FP8X4),
+                lhsT_scale=scales[:, rows],
+                rhs=w_codes[:, 2 * gate + operand, :].bitcast(FP8X4),
+                rhs_scale=w_scales[:, 2 * gate + operand, :],
+                start=(operand == 0),
+                stop=(operand == 1),
+            )
+
+        def new_sums(gate):
             sums = sums_psum.tile([P, D_H], F32, tag="sums_%d" % gate)
-            for operand in range(2):
-                rows = slice((operand * PAIR + i) * P, (operand * PAIR + i + 1) * P)
-                nc.tensor.matmul_mx(
-                    out=sums[:],
-                    lhsT=codes[:, rows].bitcast(FP8X4),
-                    lhsT_scale=scales[:, rows],
-                    rhs=w_codes[:, 2 * gate + operand, :].bitcast(FP8X4),
-                    rhs_scale=w_scales[:, 2 * gate + operand, :],
-                    start=(operand == 0),
-                    stop=(operand == 1),
-                )
             return sums
 
-        transpose_round(0)
-        for operand in range(2):
-            regroup_operand(0, operand)
+        def gate_sums(n, i, gate):
+            sums = new_sums(gate)
+            for operand in range(2):
+                multiply(sums, n, i, gate, operand)
+            return sums
+
+        def add_bias_i(sums):
+            gate_i = gates.tile([P, D_H], F32)
+            nc.vector.tensor_tensor(out=gate_i[:], in0=sums[:], in1=bias[:, 0, :], op=ADD)
+            return gate_i
+
+        def sigmoid(gate_i):
+            nc.scalar.activation(out=gate_i[:], in_=gate_i[:], func=SIGMOID)
+
+        def add_bias_c(sums):
+            result = results.tile([P, D_H], F32)
+            nc.vector.tensor_tensor(out=result[:], in0=sums[:], in1=bias[:, 1, :], op=ADD)
+            return result
+
+        def finish(n, i, gate_i, result):
+            nc.gpsimd.tensor_tensor(out=result[:], in0=result[:], in1=gate_i[:], op=MULT)
+            nc.sync.dma_start(out=out_view[n, :, i, :], in_=result[:])
 
         bias = consts.tile([P, 2, D_H], F32)
+        w_codes = consts.tile([P, 4, D_H], U32, align_bytes=64)
+        w_scales = consts.tile([P, 4, D_H], U8, align_bytes=64)
+        weight_banks = {}
+        w_grouped_tiles = {}
+
+        def transpose_weight(m):
+            weight_banks[m] = [
+                transpose_pair(weight_words[m][:, b * PAIR_WORDS : (b + 1) * PAIR_WORDS])
+                for b in range(2)
+            ]
+
+        def regroup_weight(m, *copies):
+            w_grouped = w_stage.tile([P, D_H * 4], BF16, align_bytes=64)
+            w_grouped_tiles[m] = w_grouped
+            for b, copy in enumerate(copies):
+                regroup(copy, weight_banks[m][b], w_grouped, b)
+
+        def quantise_weight(m):
+            nc.vector.quantize_mx(
+                out=w_codes[:, m, :].bitcast(FP8X4),
+                scales=w_scales[:, m, :],
+                in_=w_grouped_tiles[m][:],
+            )
+
+        S, V = nc.scalar.copy, nc.vector.tensor_copy
+        new_round(0)
+        transpose_operand(0, 0)
+        regroup_operand(0, 0)
+        transpose_weight(0)
+        quantise(0, 0, 0)
+        regroup_weight(0, S, V)
+        transpose_operand(0, 1)
+        regroup_operand(0, 1)
+        spread = [new_sums(gate) for gate in range(2)]
         for gate in range(2):
-            spread = sums_psum.tile([P, D_H], F32, tag="sums_%d" % gate)
             nc.tensor.matmul(
-                out=spread[:],
+                out=spread[gate][:],
                 lhsT=ones[:],
                 rhs=bias_rows[:, gate * D_H : (gate + 1) * D_H],
                 start=True,
                 stop=True,
             )
-            nc.vector.tensor_copy(out=bias[:, gate, :], in_=spread[:])
-        quantise_round(0)
-
-        w_codes = consts.tile([P, 4, D_H], U32, align_bytes=64)
-        w_scales = consts.tile([P, 4, D_H], U8, align_bytes=64)
-        for m in range(4):
-            w_grouped = w_stage.tile([P, D_H * 4], BF16, align_bytes=64)
-            for b, copy in enumerate((nc.scalar.copy, nc.vector.tensor_copy)):
-                bank = transpose_pair(weight_words[m][:, b * PAIR_WORDS : (b + 1) * PAIR_WORDS])
-                regroup(copy, bank, w_grouped, b)
-            nc.vector.quantize_mx(
-                out=w_codes[:, m, :].bitcast(FP8X4), scales=w_scales[:, m, :], in_=w_grouped[:]
-            )
-
+        V(out=bias[:, 0, :], in_=spread[0][:])
+        quantise_weight(0)
+        transpose_weight(1)
+        quantise(0, 1, 1)
+        S(out=bias[:, 1, :], in_=spread[1][:])
+        regroup_weight(1, S, V)
+        sums_i = [new_sums(0) for i in range(PAIR)]
+        sums_c = [new_sums(1) for i in range(PAIR)]
+        transpose_weight(2)
+        for i in range(PAIR):
+            multiply(sums_i[i], 0, i, 0, 0)
+        regroup_weight(2, S, V)
+        quantise_weight(1)
+        transpose_weight(3)
+        for i in range(PAIR):
+            multiply(sums_i[i], 0, i, 0, 1)
+        quantise_weight(2)
+        regroup_weight(3, S, S)
         transpose_round(1)
-        for operand in range(2):
-            regroup_operand(1, operand)
+        for i in range(PAIR):
+            multiply(sums_c[i], 0, i, 1, 0)
+        gates_0 = [add_bias_i(sums_i[0])]
+        quantise_weight(3)
+        gates_0.append(add_bias_i(sums_i[1]))
+        regroup_operand(1, 0)
+        regroup_operand(1, 1)
+        for gate_i in gates_0:
+            sigmoid(gate_i)
+        for i in range(PAIR):
+            multiply(sums_c[i], 0, i, 1, 1)
+        quantise_round(1)
+        transpose_round(2)
+        regroup_operand(2, 0)
+        regroup_operand(2, 1)
+        for i in range(PAIR):
+            finish(0, i, gates_0[i], add_bias_c(sums_c[i]))
 
-        for n in range(N_ROUNDS):
+        for n in range(1, N_ROUNDS):
             if n + 1 < N_ROUNDS:
                 quantise_round(n + 1)
             sums = [(gate_sums(n, 0, 0), gate_sums(n, 0, 1))]
@@ -171,12 +264,8 @@ def tile_lstmcell_pa_t_kernel(
                 transpose_round(n + 2)
             sums.append((gate_sums(n, 1, 0), gate_sums(n, 1, 1)))
             for i, (sums_i, sums_c) in enumerate(sums):
-                gate_i = gates.tile([P, D_H], F32)
-                nc.vector.tensor_tensor(out=gate_i[:], in0=sums_i[:], in1=bias[:, 0, :], op=ADD)
+                gate_i = add_bias_i(sums_i)
                 if n + 2 < N_ROUNDS:
                     regroup_operand(n + 2, i)
-                nc.scalar.activation(out=gate_i[:], in_=gate_i[:], func=SIGMOID)
-                result = results.tile([P, D_H], F32)
-                nc.vector.tensor_tensor(out=result[:], in0=sums_c[:], in1=bias[:, 1, :], op=ADD)
-                nc.gpsimd.tensor_tensor(out=result[:], in0=result[:], in1=gate_i[:], op=MULT)
-                nc.sync.dma_start(out=out_view[n, :, i, :], in_=result[:])
+                sigmoid(gate_i)
+                finish(n, i, gate_i, add_bias_c(sums_c))

@@ -33,8 +33,8 @@ def tile_lstmcell_pa_t_kernel(
         acts = ctx.enter_context(tc.tile_pool(name="acts", bufs=N_ROUNDS))
         w_stage = ctx.enter_context(tc.tile_pool(name="w_stage", bufs=4))
         quant = ctx.enter_context(tc.tile_pool(name="quant", bufs=3))
-        gates = ctx.enter_context(tc.tile_pool(name="gates", bufs=4))
-        results = ctx.enter_context(tc.tile_pool(name="results", bufs=10))
+        gates = ctx.enter_context(tc.tile_pool(name="gates", bufs=3))
+        results = ctx.enter_context(tc.tile_pool(name="results", bufs=6))
         words_psum = ctx.enter_context(tc.psum_pool(name="words_psum", bufs=4))
         sums_psum = ctx.enter_context(tc.psum_pool(name="sums_psum", bufs=2))
         ctx.enter_context(tc.manual_schedule())
@@ -159,22 +159,20 @@ def tile_lstmcell_pa_t_kernel(
                 multiply(sums, n, i, gate, operand)
             return sums
 
-        def add_bias_i(sums):
-            gate_i = gates.tile([P, D_H], F32)
-            nc.vector.tensor_tensor(out=gate_i[:], in0=sums[:], in1=bias[:, 0, :], op=ADD)
-            return gate_i
+        def round_tiles():
+            gate_i = gates.tile([P, PAIR, D_H], F32)
+            result = results.tile([P, PAIR, D_H], F32)
+            return gate_i, result
+
+        def add_bias(sums, gate, into):
+            nc.vector.tensor_tensor(out=into, in0=sums[:], in1=bias[:, gate, :], op=ADD)
 
         def sigmoid(gate_i):
-            nc.scalar.activation(out=gate_i[:], in_=gate_i[:], func=SIGMOID)
+            nc.scalar.activation(out=gate_i, in_=gate_i, func=SIGMOID)
 
-        def add_bias_c(sums):
-            result = results.tile([P, D_H], F32)
-            nc.vector.tensor_tensor(out=result[:], in0=sums[:], in1=bias[:, 1, :], op=ADD)
-            return result
-
-        def finish(n, i, gate_i, result):
+        def finish(n, gate_i, result):
             nc.gpsimd.tensor_tensor(out=result[:], in0=result[:], in1=gate_i[:], op=MULT)
-            nc.sync.dma_start(out=out_view[n, :, i, :], in_=result[:])
+            nc.sync.dma_start(out=out_view[n], in_=result[:])
 
         bias = consts.tile([P, 2, D_H], F32)
         w_codes = consts.tile([P, 4, D_H], U32, align_bytes=64)
@@ -240,13 +238,14 @@ def tile_lstmcell_pa_t_kernel(
         transpose_round(1)
         for i in range(PAIR):
             multiply(sums_c[i], 0, i, 1, 0)
-        gates_0 = [add_bias_i(sums_i[0])]
+        gate_i, result = round_tiles()
+        add_bias(sums_i[0], 0, gate_i[:, 0, :])
         quantise_weight(3)
-        gates_0.append(add_bias_i(sums_i[1]))
+        add_bias(sums_i[1], 0, gate_i[:, 1, :])
         regroup_operand(1, 0)
         regroup_operand(1, 1)
-        for gate_i in gates_0:
-            sigmoid(gate_i)
+        for i in range(PAIR):
+            sigmoid(gate_i[:, i, :])
         for i in range(PAIR):
             multiply(sums_c[i], 0, i, 1, 1)
         quantise_round(1)
@@ -254,7 +253,8 @@ def tile_lstmcell_pa_t_kernel(
         regroup_operand(2, 0)
         regroup_operand(2, 1)
         for i in range(PAIR):
-            finish(0, i, gates_0[i], add_bias_c(sums_c[i]))
+            add_bias(sums_c[i], 1, result[:, i, :])
+        finish(0, gate_i, result)
 
         for n in range(1, N_ROUNDS):
             if n + 1 < N_ROUNDS:
@@ -263,9 +263,17 @@ def tile_lstmcell_pa_t_kernel(
             if n + 2 < N_ROUNDS:
                 transpose_round(n + 2)
             sums.append((gate_sums(n, 1, 0), gate_sums(n, 1, 1)))
+            gate_i, result = round_tiles()
             for i, (sums_i, sums_c) in enumerate(sums):
-                gate_i = add_bias_i(sums_i)
+                add_bias(sums_i, 0, gate_i[:, i, :])
                 if n + 2 < N_ROUNDS:
                     regroup_operand(n + 2, i)
-                sigmoid(gate_i)
-                finish(n, i, gate_i, add_bias_c(sums_c))
+                sigmoid(gate_i[:, i, :])
+                add_bias(sums_c, 1, result[:, i, :])
+            if n < N_ROUNDS - 1:
+                finish(n, gate_i, result)
+        for i, multiplier in enumerate((nc.gpsimd, nc.vector)):
+            multiplier.tensor_tensor(
+                out=result[:, i, :], in0=result[:, i, :], in1=gate_i[:, i, :], op=MULT
+            )
+            nc.sync.dma_start(out=out_view[n, :, i, :], in_=result[:, i, :])

@@ -208,6 +208,10 @@ def tile_lstmcell_pa_t_kernel(
         regroup_weight(0, S, V)
         transpose_operand(0, 1)
         regroup_operand(0, 1)
+        quantise_weight(0)
+        transpose_weight(1)
+        quantise(0, 1, 1)
+        regroup_weight(1, S, V)
         spread = [new_sums(gate) for gate in range(2)]
         for gate in range(2):
             nc.tensor.matmul(
@@ -217,18 +221,14 @@ def tile_lstmcell_pa_t_kernel(
                 start=True,
                 stop=True,
             )
-        V(out=bias[:, 0, :], in_=spread[0][:])
-        quantise_weight(0)
-        transpose_weight(1)
-        quantise(0, 1, 1)
-        S(out=bias[:, 1, :], in_=spread[1][:])
-        regroup_weight(1, S, V)
         sums_i = [new_sums(0) for i in range(PAIR)]
         sums_c = [new_sums(1) for i in range(PAIR)]
+        S(out=bias[:, 0, :], in_=spread[0][:])
+        S(out=bias[:, 1, :], in_=spread[1][:])
         transpose_weight(2)
         for i in range(PAIR):
             multiply(sums_i[i], 0, i, 0, 0)
-        regroup_weight(2, S, V)
+        regroup_weight(2, S, S)
         quantise_weight(1)
         transpose_weight(3)
         for i in range(PAIR):
@@ -245,19 +245,20 @@ def tile_lstmcell_pa_t_kernel(
         regroup_operand(1, 0)
         regroup_operand(1, 1)
         for i in range(PAIR):
-            sigmoid(gate_i[:, i, :])
-        for i in range(PAIR):
             multiply(sums_c[i], 0, i, 1, 1)
         quantise_round(1)
         transpose_round(2)
         regroup_operand(2, 0)
         regroup_operand(2, 1)
         for i in range(PAIR):
+            sigmoid(gate_i[:, i, :])
+        for i in range(PAIR):
             add_bias(sums_c[i], 1, result[:, i, :])
+        quantise_round(2)
         finish(0, gate_i, result)
 
         for n in range(1, N_ROUNDS):
-            if n + 1 < N_ROUNDS:
+            if 1 < n < N_ROUNDS - 1:
                 quantise_round(n + 1)
             sums = [(gate_sums(n, 0, 0), gate_sums(n, 0, 1))]
             if n + 2 < N_ROUNDS:
@@ -270,10 +271,12 @@ def tile_lstmcell_pa_t_kernel(
                     regroup_operand(n + 2, i)
                 sigmoid(gate_i[:, i, :])
                 add_bias(sums_c, 1, result[:, i, :])
-            if n < N_ROUNDS - 1:
+            if n < N_ROUNDS - 2:
                 finish(n, gate_i, result)
-        for i, multiplier in enumerate((nc.gpsimd, nc.vector)):
-            multiplier.tensor_tensor(
-                out=result[:, i, :], in0=result[:, i, :], in1=gate_i[:, i, :], op=MULT
-            )
-            nc.sync.dma_start(out=out_view[n, :, i, :], in_=result[:, i, :])
+                continue
+            multiplier = nc.gpsimd if n == N_ROUNDS - 2 else nc.vector
+            for i in range(PAIR):
+                multiplier.tensor_tensor(
+                    out=result[:, i, :], in0=result[:, i, :], in1=gate_i[:, i, :], op=MULT
+                )
+                nc.sync.dma_start(out=out_view[n, :, i, :], in_=result[:, i, :])

@@ -41,7 +41,7 @@ def tile_lstmcell_pa_t_kernel(
 
         ident = consts.tile([P, P], F32)
         masks.make_identity(nc, ident[:])
-        ones = consts.tile([P, P], BF16)
+        ones = consts.tile([P, D_H], BF16)
         nc.vector.memset(ones[:], 1.0)
         bias_rows = consts.tile([P, 2 * D_H], BF16)
         nc.vector.memset(bias_rows[:], 0.0)
@@ -200,12 +200,23 @@ def tile_lstmcell_pa_t_kernel(
             )
 
         S, V = nc.scalar.copy, nc.vector.tensor_copy
+        warm_up = new_sums(0)
+
+        def keep_clock(count):
+            for repeat in range(count):
+                nc.tensor.matmul(
+                    out=warm_up[:], lhsT=ones[:, 0:P], rhs=ones[:], start=True, stop=True
+                )
+
+        keep_clock(5)
         new_round(0)
         transpose_operand(0, 0)
         regroup_operand(0, 0)
+        keep_clock(2)
         transpose_weight(0)
         quantise(0, 0, 0)
         regroup_weight(0, S, V)
+        keep_clock(2)
         transpose_operand(0, 1)
         regroup_operand(0, 1)
         quantise_weight(0)
@@ -216,7 +227,7 @@ def tile_lstmcell_pa_t_kernel(
         for gate in range(2):
             nc.tensor.matmul(
                 out=spread[gate][:],
-                lhsT=ones[:],
+                lhsT=ones[:, 0:P],
                 rhs=bias_rows[:, gate * D_H : (gate + 1) * D_H],
                 start=True,
                 stop=True,

@@ -41,7 +41,7 @@ def tile_lstmcell_pa_t_kernel(
 
         ident = consts.tile([P, P], F32)
         masks.make_identity(nc, ident[:])
-        ones = consts.tile([P, D_H], BF16)
+        ones = consts.tile([P, 2 * P], BF16)
         nc.vector.memset(ones[:], 1.0)
         bias_rows = consts.tile([P, 2 * D_H], BF16)
         nc.vector.memset(bias_rows[:], 0.0)
@@ -68,7 +68,7 @@ def tile_lstmcell_pa_t_kernel(
             w_rows = w_stage.tile([P, (D_H // P) * K], BF16)
             nc.sync.dma_start(
                 out=w_rows[:].rearrange("p (r k) -> p r k", k=K),
-                in_=w.rearrange("(r p) k -> p r k", p=P),
+                in_=w.rearrange("(p r) k -> p r k", p=P),
             )
             weight_words.append(w_rows[:].bitcast(F32))
 
@@ -165,7 +165,12 @@ def tile_lstmcell_pa_t_kernel(
             return gate_i, result
 
         def add_bias(sums, gate, into):
-            nc.vector.tensor_tensor(out=into, in0=sums[:], in1=bias[:, gate, :], op=ADD)
+            nc.vector.tensor_tensor(
+                out=into.rearrange("q (p r) -> q p r", p=P),
+                in0=sums[:].rearrange("q (r p) -> q p r", p=P),
+                in1=bias[:, gate, :].rearrange("q (p r) -> q p r", p=P),
+                op=ADD,
+            )
 
         def sigmoid(gate_i):
             nc.scalar.activation(out=gate_i, in_=gate_i, func=SIGMOID)
@@ -205,18 +210,22 @@ def tile_lstmcell_pa_t_kernel(
         def keep_clock(count):
             for repeat in range(count):
                 nc.tensor.matmul(
-                    out=warm_up[:], lhsT=ones[:, 0:P], rhs=ones[:], start=True, stop=True
+                    out=warm_up[:, 0 : 2 * P],
+                    lhsT=ones[:, 0:P],
+                    rhs=ones[:],
+                    start=True,
+                    stop=True,
                 )
 
-        keep_clock(5)
+        keep_clock(7)
         new_round(0)
         transpose_operand(0, 0)
         regroup_operand(0, 0)
-        keep_clock(2)
+        keep_clock(4)
         transpose_weight(0)
         quantise(0, 0, 0)
         regroup_weight(0, S, V)
-        keep_clock(2)
+        keep_clock(4)
         transpose_operand(0, 1)
         regroup_operand(0, 1)
         quantise_weight(0)

@@ -30,11 +30,12 @@ def tile_lstmcell_pa_t_kernel(
     nc = tc.nc
     with ExitStack() as ctx:
         consts = ctx.enter_context(tc.tile_pool(name="consts", bufs=1))
-        acts = ctx.enter_context(tc.tile_pool(name="acts", bufs=N_ROUNDS))
+        acts = ctx.enter_context(tc.tile_pool(name="acts", bufs=10))
         w_stage = ctx.enter_context(tc.tile_pool(name="w_stage", bufs=4))
+        w_quant = ctx.enter_context(tc.tile_pool(name="w_quant", bufs=2))
         quant = ctx.enter_context(tc.tile_pool(name="quant", bufs=3))
-        gates = ctx.enter_context(tc.tile_pool(name="gates", bufs=3))
-        results = ctx.enter_context(tc.tile_pool(name="results", bufs=6))
+        gates = ctx.enter_context(tc.tile_pool(name="gates", bufs=N_ROUNDS))
+        results = ctx.enter_context(tc.tile_pool(name="results", bufs=N_ROUNDS))
         words_psum = ctx.enter_context(tc.psum_pool(name="words_psum", bufs=4))
         sums_psum = ctx.enter_context(tc.psum_pool(name="sums_psum", bufs=2))
         ctx.enter_context(tc.manual_schedule())
@@ -192,7 +193,7 @@ def tile_lstmcell_pa_t_kernel(
             ]
 
         def regroup_weight(m, *copies):
-            w_grouped = w_stage.tile([P, D_H * 4], BF16, align_bytes=64)
+            w_grouped = w_quant.tile([P, D_H * 4], BF16, align_bytes=64)
             w_grouped_tiles[m] = w_grouped
             for b, copy in enumerate(copies):
                 regroup(copy, weight_banks[m][b], w_grouped, b)

@@ -34,8 +34,9 @@ def tile_lstmcell_pa_t_kernel(
         w_stage = ctx.enter_context(tc.tile_pool(name="w_stage", bufs=4))
         w_quant = ctx.enter_context(tc.tile_pool(name="w_quant", bufs=2))
         quant = ctx.enter_context(tc.tile_pool(name="quant", bufs=3))
-        gates = ctx.enter_context(tc.tile_pool(name="gates", bufs=N_ROUNDS))
+        gates = ctx.enter_context(tc.tile_pool(name="gates", bufs=N_ROUNDS - 2))
         results = ctx.enter_context(tc.tile_pool(name="results", bufs=N_ROUNDS))
+        lastp = ctx.enter_context(tc.tile_pool(name="lastp", bufs=2))
         words_psum = ctx.enter_context(tc.psum_pool(name="words_psum", bufs=4))
         sums_psum = ctx.enter_context(tc.psum_pool(name="sums_psum", bufs=2))
         ctx.enter_context(tc.manual_schedule())
@@ -49,6 +50,9 @@ def tile_lstmcell_pa_t_kernel(
         for row, (b_i, b_c) in enumerate(((b_W_i, b_W_c), (b_U_i, b_U_c))):
             nc.scalar.dma_start(out=bias_rows[row : row + 1, 0:D_H], in_=b_i.unsqueeze(0))
             nc.scalar.dma_start(out=bias_rows[row : row + 1, D_H : 2 * D_H], in_=b_c.unsqueeze(0))
+        bias_columns_w = consts.tile([P, D_H // P], BF16)
+        bias_columns_u = consts.tile([P, D_H // P], BF16)
+        bias_columns = consts.tile([P, D_H // P], F32)
         table_warmer = consts.tile([P, 1], F32)
         nc.vector.memset(table_warmer[:], 0.0)
         nc.scalar.activation(out=table_warmer[:], in_=table_warmer[:], func=SIGMOID)
@@ -82,8 +86,15 @@ def tile_lstmcell_pa_t_kernel(
                 for w in (U_i, W_c, U_c):
                     load_weight(w)
 
-        def transpose_pair(words):
+        for columns, b_gate in ((bias_columns_w, b_W_i), (bias_columns_u, b_U_i)):
+            nc.sync.dma_start(out=columns[:], in_=b_gate.rearrange("(p r) -> p r", p=P))
+
+        def new_bank():
             bank = words_psum.tile([P, 2, PAIR_ROWS], F32)
+            return bank
+
+        def transpose_pair(words):
+            bank = new_bank()
             for s in range(PAIR):
                 for u in range(2):
                     nc.tensor.transpose(
@@ -249,7 +260,7 @@ def tile_lstmcell_pa_t_kernel(
         transpose_weight(2)
         for i in range(PAIR):
             multiply(sums_i[i], 0, i, 0, 0)
-        regroup_weight(2, S, S)
+        regroup_weight(2, V, S)
         quantise_weight(1)
         transpose_weight(3)
         for i in range(PAIR):
@@ -278,26 +289,109 @@ def tile_lstmcell_pa_t_kernel(
         quantise_round(2)
         finish(0, gate_i, result)
 
-        for n in range(1, N_ROUNDS):
-            if 1 < n < N_ROUNDS - 1:
-                quantise_round(n + 1)
+        def round_sums(n):
             sums = [(gate_sums(n, 0, 0), gate_sums(n, 0, 1))]
             if n + 2 < N_ROUNDS:
                 transpose_round(n + 2)
             sums.append((gate_sums(n, 1, 0), gate_sums(n, 1, 1)))
+            return sums
+
+        def gates_of(n, i, sums, gate_i, result):
+            add_bias(sums[0], 0, gate_i[:, i, :])
+            if n + 2 < N_ROUNDS:
+                regroup_operand(n + 2, i)
+            sigmoid(gate_i[:, i, :])
+            add_bias(sums[1], 1, result[:, i, :])
+
+        for n in range(1, N_ROUNDS - 2):
+            if n > 1:
+                quantise_round(n + 1)
+            sums = round_sums(n)
             gate_i, result = round_tiles()
-            for i, (sums_i, sums_c) in enumerate(sums):
-                add_bias(sums_i, 0, gate_i[:, i, :])
-                if n + 2 < N_ROUNDS:
-                    regroup_operand(n + 2, i)
-                sigmoid(gate_i[:, i, :])
-                add_bias(sums_c, 1, result[:, i, :])
-            if n < N_ROUNDS - 2:
-                finish(n, gate_i, result)
-                continue
-            multiplier = nc.gpsimd if n == N_ROUNDS - 2 else nc.vector
             for i in range(PAIR):
-                multiplier.tensor_tensor(
-                    out=result[:, i, :], in0=result[:, i, :], in1=gate_i[:, i, :], op=MULT
+                gates_of(n, i, sums[i], gate_i, result)
+            finish(n, gate_i, result)
+            if n == N_ROUNDS // 2:
+                nc.gpsimd.tensor_tensor(
+                    out=bias_columns[:], in0=bias_columns_w[:], in1=bias_columns_u[:], op=ADD
+                )
+
+        def feature_sums(n):
+            codes, scales = packed[n]
+            banks = []
+            for half in range(2):
+                bank = new_bank()
+                banks.append(bank)
+                for j in range(2):
+                    features = slice((2 * half + j) * P, (2 * half + j + 1) * P)
+                    for operand in range(2):
+                        rows = slice(operand * PAIR_ROWS, (operand + 1) * PAIR_ROWS)
+                        nc.tensor.matmul_mx(
+                            out=bank[:, j, :],
+                            lhsT=w_codes[:, operand, features].bitcast(FP8X4),
+                            lhsT_scale=w_scales[:, operand, features],
+                            rhs=codes[:, rows].bitcast(FP8X4),
+                            rhs_scale=scales[:, rows],
+                            start=(operand == 0),
+                            stop=(operand == 1),
+                        )
+            return banks
+
+        def feature_gate(banks):
+            gate_f = lastp.tile([P, D_H // P, PAIR_ROWS], F32)
+            for r in range(D_H // P):
+                nc.scalar.activation(
+                    out=gate_f[:, r, :],
+                    in_=banks[r // 2][:, r % 2, :],
+                    func=SIGMOID,
+                    bias=bias_columns[:, r : r + 1],
+                )
+            return gate_f
+
+        def candidate_sums(n):
+            pair = []
+            for i in range(PAIR):
+                sums_c = new_sums(1 - i)
+                for operand in range(2):
+                    multiply(sums_c, n, i, 1, operand)
+                pair.append(sums_c)
+            return pair
+
+        def turn_gate(gate_f):
+            banks = []
+            for i in range(PAIR):
+                bank = new_bank()
+                banks.append(bank)
+                for r in range(D_H // P):
+                    nc.tensor.transpose(
+                        out=bank[:, r // 2, (r % 2) * P : (r % 2 + 1) * P],
+                        in_=gate_f[:, r, i * P : (i + 1) * P],
+                        identity=ident[:],
+                    )
+            return banks
+
+        def last_product(n, sums_c, gate_banks):
+            result = results.tile([P, PAIR, D_H], F32)
+            for i in range(PAIR):
+                add_bias(sums_c[i], 1, result[:, i, :])
+            for i in range(PAIR):
+                nc.vector.tensor_tensor(
+                    out=result[:, i, :].rearrange("q (p r) -> q p r", p=P),
+                    in0=result[:, i, :].rearrange("q (p r) -> q p r", p=P),
+                    in1=gate_banks[i][:].rearrange("q a (b p) -> q p (a b)", p=P),
+                    op=MULT,
                 )
                 nc.sync.dma_start(out=out_view[n, :, i, :], in_=result[:, i, :])
+
+        n, last = N_ROUNDS - 2, N_ROUNDS - 1
+        quantise_round(last)
+        banks = feature_sums(n)
+        gate_f = feature_gate(banks)
+        sums_c = candidate_sums(n)
+        last_banks = feature_sums(last)
+        turned = turn_gate(gate_f)
+        last_gate_f = feature_gate(last_banks)
+        last_sums_c = candidate_sums(last)
+        last_product(n, sums_c, turned)
+        turned = turn_gate(last_gate_f)
+        last_product(last, last_sums_c, turned)

@@ -276,16 +276,16 @@ def tile_lstmcell_pa_t_kernel(
         add_bias(sums_i[1], 0, gate_i[:, 1, :])
         regroup_operand(1, 0)
         regroup_operand(1, 1)
+        transpose_round(2)
         for i in range(PAIR):
             multiply(sums_c[i], 0, i, 1, 1)
         quantise_round(1)
-        transpose_round(2)
         regroup_operand(2, 0)
         regroup_operand(2, 1)
         for i in range(PAIR):
             sigmoid(gate_i[:, i, :])
-        for i in range(PAIR):
-            add_bias(sums_c[i], 1, result[:, i, :])
+        add_bias(sums_c[0], 1, result[:, 0, :])
+        add_bias(sums_c[1], 1, result[:, 1, :])
         quantise_round(2)
         finish(0, gate_i, result)
 

from contextlib import ExitStack

import concourse.masks as masks
import concourse.mybir as mybir

F32 = mybir.dt.float32
BF16 = mybir.dt.bfloat16
U32 = mybir.dt.uint32
U8 = mybir.dt.uint8
FP8X4 = mybir.dt.float8_e4m3fn_x4
ADD = mybir.AluOpType.add
MULT = mybir.AluOpType.mult
SIGMOID = mybir.ActivationFunctionType.Sigmoid

P = 128
BATCH = 4096
K = 512
D_H = 512
PAIR = 2
PAIR_ROWS = PAIR * P
PAIR_WORDS = PAIR * K // 2
N_ROUNDS = BATCH // PAIR_ROWS

FLOPS = 2 * BATCH * K * D_H * 4


def tile_lstmcell_pa_t_kernel(
    tc, incoming, h, W_i, b_W_i, W_c, b_W_c, U_i, b_U_i, U_c, b_U_c, out
):
    nc = tc.nc
    with ExitStack() as ctx:
        consts = ctx.enter_context(tc.tile_pool(name="consts", bufs=1))
        acts = ctx.enter_context(tc.tile_pool(name="acts", bufs=10))
        w_stage = ctx.enter_context(tc.tile_pool(name="w_stage", bufs=4))
        w_quant = ctx.enter_context(tc.tile_pool(name="w_quant", bufs=2))
        quant = ctx.enter_context(tc.tile_pool(name="quant", bufs=3))
        gates = ctx.enter_context(tc.tile_pool(name="gates", bufs=N_ROUNDS - 2))
        results = ctx.enter_context(tc.tile_pool(name="results", bufs=N_ROUNDS))
        lastp = ctx.enter_context(tc.tile_pool(name="lastp", bufs=2))
        words_psum = ctx.enter_context(tc.psum_pool(name="words_psum", bufs=4))
        sums_psum = ctx.enter_context(tc.psum_pool(name="sums_psum", bufs=2))
        ctx.enter_context(tc.manual_schedule())

        ident = consts.tile([P, P], F32)
        masks.make_identity(nc, ident[:])
        ones = consts.tile([P, 2 * P], BF16)
        nc.vector.memset(ones[:], 1.0)
        bias_rows = consts.tile([P, 2 * D_H], BF16)
        nc.vector.memset(bias_rows[:], 0.0)
        for row, (b_i, b_c) in enumerate(((b_W_i, b_W_c), (b_U_i, b_U_c))):
            nc.scalar.dma_start(out=bias_rows[row : row + 1, 0:D_H], in_=b_i.unsqueeze(0))
            nc.scalar.dma_start(out=bias_rows[row : row + 1, D_H : 2 * D_H], in_=b_c.unsqueeze(0))
        bias_columns_w = consts.tile([P, D_H // P], BF16)
        bias_columns_u = consts.tile([P, D_H // P], BF16)
        bias_columns = consts.tile([P, D_H // P], F32)
        table_warmer = consts.tile([P, 1], F32)
        nc.vector.memset(table_warmer[:], 0.0)
        nc.scalar.activation(out=table_warmer[:], in_=table_warmer[:], func=SIGMOID)

        x_view = incoming.rearrange("(n p i) k -> n p (i k)", p=P, i=PAIR)
        h_view = h.rearrange("(n p i) k -> n p (i k)", p=P, i=PAIR)
        out_view = out.rearrange("(n p i) f -> n p i f", p=P, i=PAIR)
        act_words = {}

        def load_operand(n, operand):
            rows = acts.tile([P, PAIR * K], BF16, name="rows_%d" % operand)
            nc.sync.dma_start(out=rows[:], in_=(x_view, h_view)[operand][n])
            act_words.setdefault(n, []).append(rows[:].bitcast(F32))

        weight_words = []

        def load_weight(w):
            w_rows = w_stage.tile([P, (D_H // P) * K], BF16)
            nc.sync.dma_start(
                out=w_rows[:].rearrange("p (r k) -> p r k", k=K),
                in_=w.rearrange("(p r) k -> p r k", p=P),
            )
            weight_words.append(w_rows[:].bitcast(F32))

        for n in range(N_ROUNDS):
            load_operand(n, 0)
            if n == 0:
                load_weight(W_i)
            load_operand(n, 1)
            if n == 0:
                for w in (U_i, W_c, U_c):
                    load_weight(w)

        for columns, b_gate in ((bias_columns_w, b_W_i), (bias_columns_u, b_U_i)):
            nc.sync.dma_start(out=columns[:], in_=b_gate.rearrange("(p r) -> p r", p=P))

        def new_bank():
            bank = words_psum.tile([P, 2, PAIR_ROWS], F32)
            return bank

        def transpose_pair(words):
            bank = new_bank()
            for s in range(PAIR):
                for u in range(2):
                    nc.tensor.transpose(
                        out=bank[:, u, s * P : (s + 1) * P],
                        in_=words[:, 2 * s * P + u : 2 * (s + 1) * P : 2],
                        identity=ident[:],
                    )
            return bank

        def regroup(copy, bank, grouped, b):
            copy(
                out=grouped[:]
                .bitcast(F32)[:, b * PAIR_WORDS : (b + 1) * PAIR_WORDS]
                .rearrange("p (r u) -> p r u", u=2),
                in_=bank[:].rearrange("p u r -> p r u"),
            )

        word_banks = {}
        grouped_tiles = {}
        packed = {}

        def new_round(n):
            word_banks[n] = {}
            grouped_tiles[n] = quant.tile(
                [P, 2 * PAIR_ROWS * 4], BF16, align_bytes=64, name="grouped"
            )
            codes = quant.tile([P, 2 * PAIR_ROWS], U32, align_bytes=64)
            scales = quant.tile([P, 2 * PAIR_ROWS], U8, align_bytes=64)
            packed[n] = (codes, scales)

        def transpose_operand(n, operand):
            word_banks[n][operand] = transpose_pair(act_words[n][operand])

        def transpose_round(n):
            new_round(n)
            for operand in range(2):
                transpose_operand(n, operand)

        def regroup_operand(n, operand):
            regroup(nc.scalar.copy, word_banks[n][operand], grouped_tiles[n], operand)

        def quantise(n, first, last):
            codes, scales = packed[n]
            cols = slice(first * PAIR_ROWS, (last + 1) * PAIR_ROWS)
            nc.vector.quantize_mx(
                out=codes[:, cols].bitcast(FP8X4),
                scales=scales[:, cols],
                in_=grouped_tiles[n][:, cols.start * 4 : cols.stop * 4],
            )

        def quantise_round(n):
            quantise(n, 0, 1)

        def multiply(sums, n, i, gate, operand):
            codes, scales = packed[n]
            rows = slice((operand * PAIR + i) * P, (operand * PAIR + i + 1) * P)
            nc.tensor.matmul_mx(
                out=sums[:],
                lhsT=codes[:, rows].bitcast(FP8X4),
                lhsT_scale=scales[:, rows],
                rhs=w_codes[:, 2 * gate + operand, :].bitcast(FP8X4),
                rhs_scale=w_scales[:, 2 * gate + operand, :],
                start=(operand == 0),
                stop=(operand == 1),
            )

        def new_sums(gate):
            sums = sums_psum.tile([P, D_H], F32, tag="sums_%d" % gate)
            return sums

        def gate_sums(n, i, gate):
            sums = new_sums(gate)
            for operand in range(2):
                multiply(sums, n, i, gate, operand)
            return sums

        def round_tiles():
            gate_i = gates.tile([P, PAIR, D_H], F32)
            result = results.tile([P, PAIR, D_H], F32)
            return gate_i, result

        def add_bias(sums, gate, into):
            nc.vector.tensor_tensor(
                out=into.rearrange("q (p r) -> q p r", p=P),
                in0=sums[:].rearrange("q (r p) -> q p r", p=P),
                in1=bias[:, gate, :].rearrange("q (p r) -> q p r", p=P),
                op=ADD,
            )

        def sigmoid(gate_i):
            nc.scalar.activation(out=gate_i, in_=gate_i, func=SIGMOID)

        def finish(n, gate_i, result):
            nc.gpsimd.tensor_tensor(out=result[:], in0=result[:], in1=gate_i[:], op=MULT)
            nc.sync.dma_start(out=out_view[n], in_=result[:])

        bias = consts.tile([P, 2, D_H], F32)
        w_codes = consts.tile([P, 4, D_H], U32, align_bytes=64)
        w_scales = consts.tile([P, 4, D_H], U8, align_bytes=64)
        weight_banks = {}
        w_grouped_tiles = {}

        def transpose_weight(m):
            weight_banks[m] = [
                transpose_pair(weight_words[m][:, b * PAIR_WORDS : (b + 1) * PAIR_WORDS])
                for b in range(2)
            ]

        def regroup_weight(m, *copies):
            w_grouped = w_quant.tile([P, D_H * 4], BF16, align_bytes=64)
            w_grouped_tiles[m] = w_grouped
            for b, copy in enumerate(copies):
                regroup(copy, weight_banks[m][b], w_grouped, b)

        def quantise_weight(m):
            nc.vector.quantize_mx(
                out=w_codes[:, m, :].bitcast(FP8X4),
                scales=w_scales[:, m, :],
                in_=w_grouped_tiles[m][:],
            )

        S, V = nc.scalar.copy, nc.vector.tensor_copy
        warm_up = new_sums(0)

        def keep_clock(count):
            for repeat in range(count):
                nc.tensor.matmul(
                    out=warm_up[:, 0 : 2 * P],
                    lhsT=ones[:, 0:P],
                    rhs=ones[:],
                    start=True,
                    stop=True,
                )

        keep_clock(7)
        new_round(0)
        transpose_operand(0, 0)
        regroup_operand(0, 0)
        keep_clock(4)
        transpose_weight(0)
        quantise(0, 0, 0)
        regroup_weight(0, S, V)
        keep_clock(4)
        transpose_operand(0, 1)
        regroup_operand(0, 1)
        quantise_weight(0)
        transpose_weight(1)
        quantise(0, 1, 1)
        regroup_weight(1, S, V)
        spread = [new_sums(gate) for gate in range(2)]
        for gate in range(2):
            nc.tensor.matmul(
                out=spread[gate][:],
                lhsT=ones[:, 0:P],
                rhs=bias_rows[:, gate * D_H : (gate + 1) * D_H],
                start=True,
                stop=True,
            )
        sums_i = [new_sums(0) for i in range(PAIR)]
        sums_c = [new_sums(1) for i in range(PAIR)]
        S(out=bias[:, 0, :], in_=spread[0][:])
        S(out=bias[:, 1, :], in_=spread[1][:])
        transpose_weight(2)
        for i in range(PAIR):
            multiply(sums_i[i], 0, i, 0, 0)
        regroup_weight(2, V, S)
        quantise_weight(1)
        transpose_weight(3)
        for i in range(PAIR):
            multiply(sums_i[i], 0, i, 0, 1)
        quantise_weight(2)
        regroup_weight(3, S, S)
        transpose_round(1)
        for i in range(PAIR):
            multiply(sums_c[i], 0, i, 1, 0)
        gate_i, result = round_tiles()
        add_bias(sums_i[0], 0, gate_i[:, 0, :])
        quantise_weight(3)
        add_bias(sums_i[1], 0, gate_i[:, 1, :])
        regroup_operand(1, 0)
        regroup_operand(1, 1)
        transpose_round(2)
        for i in range(PAIR):
            multiply(sums_c[i], 0, i, 1, 1)
        quantise_round(1)
        regroup_operand(2, 0)
        regroup_operand(2, 1)
        for i in range(PAIR):
            sigmoid(gate_i[:, i, :])
        add_bias(sums_c[0], 1, result[:, 0, :])
        add_bias(sums_c[1], 1, result[:, 1, :])
        quantise_round(2)
        finish(0, gate_i, result)

        def round_sums(n):
            sums = [(gate_sums(n, 0, 0), gate_sums(n, 0, 1))]
            if n + 2 < N_ROUNDS:
                transpose_round(n + 2)
            sums.append((gate_sums(n, 1, 0), gate_sums(n, 1, 1)))
            return sums

        def gates_of(n, i, sums, gate_i, result):
            add_bias(sums[0], 0, gate_i[:, i, :])
            if n + 2 < N_ROUNDS:
                regroup_operand(n + 2, i)
            sigmoid(gate_i[:, i, :])
            add_bias(sums[1], 1, result[:, i, :])

        for n in range(1, N_ROUNDS - 2):
            if n > 1:
                quantise_round(n + 1)
            sums = round_sums(n)
            gate_i, result = round_tiles()
            for i in range(PAIR):
                gates_of(n, i, sums[i], gate_i, result)
            finish(n, gate_i, result)
            if n == N_ROUNDS // 2:
                nc.gpsimd.tensor_tensor(
                    out=bias_columns[:], in0=bias_columns_w[:], in1=bias_columns_u[:], op=ADD
                )

        def feature_sums(n):
            codes, scales = packed[n]
            banks = []
            for half in range(2):
                bank = new_bank()
                banks.append(bank)
                for j in range(2):
                    features = slice((2 * half + j) * P, (2 * half + j + 1) * P)
                    for operand in range(2):
                        rows = slice(operand * PAIR_ROWS, (operand + 1) * PAIR_ROWS)
                        nc.tensor.matmul_mx(
                            out=bank[:, j, :],
                            lhsT=w_codes[:, operand, features].bitcast(FP8X4),
                            lhsT_scale=w_scales[:, operand, features],
                            rhs=codes[:, rows].bitcast(FP8X4),
                            rhs_scale=scales[:, rows],
                            start=(operand == 0),
                            stop=(operand == 1),
                        )
            return banks

        def feature_gate(banks):
            gate_f = lastp.tile([P, D_H // P, PAIR_ROWS], F32)
            for r in range(D_H // P):
                nc.scalar.activation(
                    out=gate_f[:, r, :],
                    in_=banks[r // 2][:, r % 2, :],
                    func=SIGMOID,
                    bias=bias_columns[:, r : r + 1],
                )
            return gate_f

        def candidate_sums(n):
            pair = []
            for i in range(PAIR):
                sums_c = new_sums(1 - i)
                for operand in range(2):
                    multiply(sums_c, n, i, 1, operand)
                pair.append(sums_c)
            return pair

        def turn_gate(gate_f):
            banks = []
            for i in range(PAIR):
                bank = new_bank()
                banks.append(bank)
                for r in range(D_H // P):
                    nc.tensor.transpose(
                        out=bank[:, r // 2, (r % 2) * P : (r % 2 + 1) * P],
                        in_=gate_f[:, r, i * P : (i + 1) * P],
                        identity=ident[:],
                    )
            return banks

        def last_product(n, sums_c, gate_banks):
            result = results.tile([P, PAIR, D_H], F32)
            for i in range(PAIR):
                add_bias(sums_c[i], 1, result[:, i, :])
            for i in range(PAIR):
                nc.vector.tensor_tensor(
                    out=result[:, i, :].rearrange("q (p r) -> q p r", p=P),
                    in0=result[:, i, :].rearrange("q (p r) -> q p r", p=P),
                    in1=gate_banks[i][:].rearrange("q a (b p) -> q p (a b)", p=P),
                    op=MULT,
                )
                nc.sync.dma_start(out=out_view[n, :, i, :], in_=result[:, i, :])

        n, last = N_ROUNDS - 2, N_ROUNDS - 1
        quantise_round(last)
        banks = feature_sums(n)
        gate_f = feature_gate(banks)
        sums_c = candidate_sums(n)
        last_banks = feature_sums(last)
        turned = turn_gate(gate_f)
        last_gate_f = feature_gate(last_banks)
        last_sums_c = candidate_sums(last)
        last_product(n, sums_c, turned)
        turned = turn_gate(last_gate_f)
        last_product(last, last_sums_c, turned)
